import numpy as np
import ml_dtypes

BF16 = ml_dtypes.bfloat16


def bf(x):
    return np.asarray(x, np.float32).astype(BF16)


def f32(x):
    return np.asarray(x, np.float32)


def f64(x):
    return np.asarray(x).astype(np.float64)


def striped(idx):
    return np.tile(idx.reshape(-1, 16).T, (8, 1))


C, S, A, N, H, R = 128, 1024, 4, 4096, 512, 8


def sigmoid(v):
    return 1.0 / (1.0 + np.exp(-v))


def setup_inputs():
    return {"xi": f32(np.random.standard_normal((C, S))), "xo": f32(np.random.standard_normal((C, S))), "xu": f32(0.2 * np.random.standard_normal((C, S))), "xf": f32(np.random.standard_normal((C, A))), "b_i": f32(0.3 * np.random.standard_normal((C, 1))), "b_o": f32(0.3 * np.random.standard_normal((C, 1))), "b_u": f32(0.1 * np.random.standard_normal((C, 1))), "b_f": f32(0.3 * np.random.standard_normal((C, 1))), "cw": f32(0.5 + np.random.random((1, N))), "offs": striped(np.concatenate([np.random.permutation(S)[:H] for _ in range(R)]))}


def reference(xi, xo, xu, xf, b_i, b_o, b_u, b_f, cw, offs):
    idx = offs[:16].T.reshape(-1)
    gate_in = sigmoid(f64(xi) + f64(b_i))
    gate_out = sigmoid(f64(xo) + f64(b_o))
    upd = np.tanh(f64(xu) + f64(b_u))
    cell = gate_in * upd
    forget = sigmoid(f64(xf) + f64(b_f))
    fw = np.tile(forget, (1, S)) * f64(cw)
    p = cell[:, idx] * fw
    return gate_out * np.tanh(cell + p.reshape(C, S, A).sum(axis=2))

@@ -1,0 +1,80 @@
+import concourse.mybir as mybir
+
+F32 = mybir.dt.float32
+U16 = mybir.dt.uint16
+ACT = mybir.ActivationFunctionType
+ALU = mybir.AluOpType
+AXIS = mybir.AxisListType
+
+C = 128
+S = 1024
+A = 4
+N = S * A
+PIECE = S
+NODES = PIECE // A
+
+
+def tile_batchedchildsumtreelstm_kernel(tc, xi, xo, xu, xf, b_i, b_o, b_u, b_f, cw, offs, out):
+    nc = tc.nc
+    with tc.tile_pool(name="held", bufs=1) as held:
+        offsets = held.tile([C, N // 16], U16, name="offsets")
+        nc.sync.dma_start(offsets[:], offs)
+
+        pre_i = held.tile([C, S], F32, name="pre_i")
+        pre_u = held.tile([C, S], F32, name="pre_u")
+        pre_o = held.tile([C, S], F32, name="pre_o")
+        pre_f = held.tile([C, A], F32, name="pre_f")
+        bias_i = held.tile([C, 1], F32, name="bias_i")
+        bias_u = held.tile([C, 1], F32, name="bias_u")
+        bias_o = held.tile([C, 1], F32, name="bias_o")
+        bias_f = held.tile([C, 1], F32, name="bias_f")
+        child_w = held.tile([C, N], F32, name="child_w")
+        nc.gpsimd.dma_start(bias_i[:], b_i)
+        nc.gpsimd.dma_start(bias_u[:], b_u)
+        nc.gpsimd.dma_start(bias_f[:], b_f)
+        nc.gpsimd.dma_start(pre_f[:], xf)
+        nc.gpsimd.dma_start(bias_o[:], b_o)
+        nc.sync.dma_start(pre_i[:], xi)
+        nc.scalar.dma_start(pre_u[:], xu)
+        nc.sync.dma_start(child_w[:], cw.rearrange("o n -> (o n)").partition_broadcast(C))
+        nc.scalar.dma_start(pre_o[:], xo)
+
+        gate_i = held.tile([C, S], F32, name="gate_i")
+        update = held.tile([C, S], F32, name="update")
+        gate_o = held.tile([C, S], F32, name="gate_o")
+        gate_f = held.tile([C, A], F32, name="gate_f")
+        nc.scalar.activation(gate_i[:], pre_i[:], ACT.Sigmoid, bias=bias_i[:])
+        nc.scalar.activation(update[:], pre_u[:], ACT.Tanh, bias=bias_u[:])
+        nc.scalar.activation(gate_f[:], pre_f[:], ACT.Sigmoid, bias=bias_f[:])
+        nc.scalar.activation(gate_o[:], pre_o[:], ACT.Sigmoid, bias=bias_o[:])
+
+        cell = held.tile([C, S], F32, name="cell")
+        nc.vector.tensor_tensor(cell[:], gate_i[:], update[:], ALU.mult)
+
+        fw = held.tile([C, N], F32, name="fw")
+        nc.vector.tensor_tensor(
+            fw[:].rearrange("c (t a) -> c t a", a=A),
+            child_w[:].rearrange("c (t a) -> c t a", a=A),
+            gate_f[:].unsqueeze(1).to_broadcast([C, S, A]),
+            ALU.mult,
+        )
+
+        product = held.tile([C, N], F32, name="product")
+        state = held.tile([C, S], F32, name="state")
+        hidden = held.tile([C, S], F32, name="hidden")
+        for k in range(N // PIECE):
+            entries = slice(k * PIECE, (k + 1) * PIECE)
+            nodes = slice(k * NODES, (k + 1) * NODES)
+            nc.vector.tensor_tensor(
+                product[:, entries],
+                cell[:].indirect(offsets[:, k * (PIECE // 16) : (k + 1) * (PIECE // 16)]),
+                fw[:, entries],
+                ALU.mult,
+            )
+            nc.vector.tensor_reduce(
+                state[:, nodes], product[:, entries].rearrange("c (t a) -> c t a", a=A), AXIS.X, ALU.add
+            )
+            nc.vector.tensor_tensor(state[:, nodes], state[:, nodes], cell[:, nodes], ALU.add)
+            nc.scalar.activation(hidden[:, nodes], state[:, nodes], ACT.Tanh)
+            nc.vector.tensor_tensor(hidden[:, nodes], hidden[:, nodes], gate_o[:, nodes], ALU.mult)
+        nc.sync.dma_start(out, hidden[:])

@@ -11,70 +11,78 @@ S = 1024
 A = 4
 N = S * A
 PIECE = S
+PIECES = N // PIECE
 NODES = PIECE // A
+CHUNK = 256
+CHUNKS = S // CHUNK
 
 
 def tile_batchedchildsumtreelstm_kernel(tc, xi, xo, xu, xf, b_i, b_o, b_u, b_f, cw, offs, out):
     nc = tc.nc
     with tc.tile_pool(name="held", bufs=1) as held:
+        bias_i = held.tile([C, 1], F32, name="bias_i")
+        bias_u = held.tile([C, 1], F32, name="bias_u")
+        nc.sync.dma_start(bias_i[:], b_i)
+        nc.scalar.dma_start(bias_u[:], b_u)
+        pre_i = [held.tile([C, CHUNK], F32, name=f"pre_i{h}") for h in range(CHUNKS)]
+        pre_u = [held.tile([C, CHUNK], F32, name=f"pre_u{h}") for h in range(CHUNKS)]
+        for h in range(CHUNKS):
+            columns = slice(h * CHUNK, (h + 1) * CHUNK)
+            nc.sync.dma_start(pre_i[h][:], xi[:, columns])
+            nc.scalar.dma_start(pre_u[h][:], xu[:, columns])
+
         offsets = held.tile([C, N // 16], U16, name="offsets")
         nc.sync.dma_start(offsets[:], offs)
 
-        pre_i = held.tile([C, S], F32, name="pre_i")
-        pre_u = held.tile([C, S], F32, name="pre_u")
-        pre_o = held.tile([C, S], F32, name="pre_o")
-        pre_f = held.tile([C, A], F32, name="pre_f")
-        bias_i = held.tile([C, 1], F32, name="bias_i")
-        bias_u = held.tile([C, 1], F32, name="bias_u")
-        bias_o = held.tile([C, 1], F32, name="bias_o")
         bias_f = held.tile([C, 1], F32, name="bias_f")
-        child_w = held.tile([C, N], F32, name="child_w")
-        nc.gpsimd.dma_start(bias_i[:], b_i)
-        nc.gpsimd.dma_start(bias_u[:], b_u)
-        nc.gpsimd.dma_start(bias_f[:], b_f)
-        nc.gpsimd.dma_start(pre_f[:], xf)
-        nc.gpsimd.dma_start(bias_o[:], b_o)
-        nc.sync.dma_start(pre_i[:], xi)
-        nc.scalar.dma_start(pre_u[:], xu)
-        nc.sync.dma_start(child_w[:], cw.rearrange("o n -> (o n)").partition_broadcast(C))
+        pre_f = held.tile([C, A], F32, name="pre_f")
+        nc.scalar.dma_start(bias_f[:], b_f)
+        nc.scalar.dma_start(pre_f[:], xf)
+
+        child_w = [held.tile([C, PIECE], F32, name=f"child_w{k}") for k in range(PIECES)]
+        for k in range(PIECES):
+            row = cw[:, k * PIECE : (k + 1) * PIECE].rearrange("o n -> (o n)")
+            nc.sync.dma_start(child_w[k][:], row.partition_broadcast(C))
+
+        bias_o = held.tile([C, 1], F32, name="bias_o")
+        pre_o = held.tile([C, S], F32, name="pre_o")
+        nc.scalar.dma_start(bias_o[:], b_o)
         nc.scalar.dma_start(pre_o[:], xo)
 
+        cell = held.tile([C, S], F32, name="cell")
         gate_i = held.tile([C, S], F32, name="gate_i")
         update = held.tile([C, S], F32, name="update")
-        gate_o = held.tile([C, S], F32, name="gate_o")
+        for h in range(CHUNKS):
+            columns = slice(h * CHUNK, (h + 1) * CHUNK)
+            nc.scalar.activation(gate_i[:, columns], pre_i[h][:], ACT.Sigmoid, bias=bias_i[:])
+            nc.scalar.activation(update[:, columns], pre_u[h][:], ACT.Tanh, bias=bias_u[:])
+            nc.vector.tensor_tensor(cell[:, columns], gate_i[:, columns], update[:, columns], ALU.mult)
+
         gate_f = held.tile([C, A], F32, name="gate_f")
-        nc.scalar.activation(gate_i[:], pre_i[:], ACT.Sigmoid, bias=bias_i[:])
-        nc.scalar.activation(update[:], pre_u[:], ACT.Tanh, bias=bias_u[:])
+        gate_o = held.tile([C, S], F32, name="gate_o")
         nc.scalar.activation(gate_f[:], pre_f[:], ACT.Sigmoid, bias=bias_f[:])
         nc.scalar.activation(gate_o[:], pre_o[:], ACT.Sigmoid, bias=bias_o[:])
 
-        cell = held.tile([C, S], F32, name="cell")
-        nc.vector.tensor_tensor(cell[:], gate_i[:], update[:], ALU.mult)
-
-        fw = held.tile([C, N], F32, name="fw")
-        nc.vector.tensor_tensor(
-            fw[:].rearrange("c (t a) -> c t a", a=A),
-            child_w[:].rearrange("c (t a) -> c t a", a=A),
-            gate_f[:].unsqueeze(1).to_broadcast([C, S, A]),
-            ALU.mult,
-        )
-
-        product = held.tile([C, N], F32, name="product")
         state = held.tile([C, S], F32, name="state")
         hidden = held.tile([C, S], F32, name="hidden")
-        for k in range(N // PIECE):
-            entries = slice(k * PIECE, (k + 1) * PIECE)
+        for k in range(PIECES):
             nodes = slice(k * NODES, (k + 1) * NODES)
+            fw = held.tile([C, PIECE], F32, name=f"fw{k}")
             nc.vector.tensor_tensor(
-                product[:, entries],
-                cell[:].indirect(offsets[:, k * (PIECE // 16) : (k + 1) * (PIECE // 16)]),
-                fw[:, entries],
+                fw[:].rearrange("c (t a) -> c t a", a=A),
+                child_w[k][:].rearrange("c (t a) -> c t a", a=A),
+                gate_f[:].unsqueeze(1).to_broadcast([C, NODES, A]),
                 ALU.mult,
             )
-            nc.vector.tensor_reduce(
-                state[:, nodes], product[:, entries].rearrange("c (t a) -> c t a", a=A), AXIS.X, ALU.add
+            product = held.tile([C, PIECE], F32, name=f"product{k}")
+            nc.vector.tensor_tensor(
+                product[:],
+                cell[:].indirect(offsets[:, k * (PIECE // 16) : (k + 1) * (PIECE // 16)]),
+                fw[:],
+                ALU.mult,
             )
+            nc.vector.tensor_reduce(state[:, nodes], product[:].rearrange("c (t a) -> c t a", a=A), AXIS.X, ALU.add)
             nc.vector.tensor_tensor(state[:, nodes], state[:, nodes], cell[:, nodes], ALU.add)
             nc.scalar.activation(hidden[:, nodes], state[:, nodes], ACT.Tanh)
             nc.vector.tensor_tensor(hidden[:, nodes], hidden[:, nodes], gate_o[:, nodes], ALU.mult)
-        nc.sync.dma_start(out, hidden[:])
+            nc.sync.dma_start(out[:, nodes], hidden[:, nodes])

@@ -1,53 +1,61 @@
 import concourse.mybir as mybir
+from concourse.masks import make_identity
 
 F32 = mybir.dt.float32
 U16 = mybir.dt.uint16
 ACT = mybir.ActivationFunctionType
 ALU = mybir.AluOpType
-AXIS = mybir.AxisListType
 
 C = 128
 S = 1024
 A = 4
 N = S * A
-PIECE = S
+PIECE = 512
 PIECES = N // PIECE
 NODES = PIECE // A
 CHUNK = 256
 CHUNKS = S // CHUNK
+LAG = 2
 
 
 def tile_batchedchildsumtreelstm_kernel(tc, xi, xo, xu, xf, b_i, b_o, b_u, b_f, cw, offs, out):
     nc = tc.nc
-    with tc.tile_pool(name="held", bufs=1) as held:
+    with tc.tile_pool(name="held", bufs=1) as held, tc.psum_pool(name="sums", bufs=1) as sums:
+        warm = held.tile([C, 1], F32, name="warm")
+        nc.vector.memset(warm[:], 0.0)
+        nc.scalar.activation(warm[:], warm[:], ACT.Sigmoid)
+
+        identity = held.tile([C, C], F32, name="identity")
+        make_identity(nc, identity[:])
+
         bias_i = held.tile([C, 1], F32, name="bias_i")
         bias_u = held.tile([C, 1], F32, name="bias_u")
         nc.sync.dma_start(bias_i[:], b_i)
-        nc.scalar.dma_start(bias_u[:], b_u)
+        nc.sync.dma_start(bias_u[:], b_u)
         pre_i = [held.tile([C, CHUNK], F32, name=f"pre_i{h}") for h in range(CHUNKS)]
         pre_u = [held.tile([C, CHUNK], F32, name=f"pre_u{h}") for h in range(CHUNKS)]
         for h in range(CHUNKS):
             columns = slice(h * CHUNK, (h + 1) * CHUNK)
             nc.sync.dma_start(pre_i[h][:], xi[:, columns])
-            nc.scalar.dma_start(pre_u[h][:], xu[:, columns])
+            nc.sync.dma_start(pre_u[h][:], xu[:, columns])
+
+        bias_f = held.tile([C, 1], F32, name="bias_f")
+        pre_f = held.tile([C, A], F32, name="pre_f")
+        nc.sync.dma_start(bias_f[:], b_f)
+        nc.sync.dma_start(pre_f[:], xf)
 
         offsets = held.tile([C, N // 16], U16, name="offsets")
         nc.sync.dma_start(offsets[:], offs)
 
-        bias_f = held.tile([C, 1], F32, name="bias_f")
-        pre_f = held.tile([C, A], F32, name="pre_f")
-        nc.scalar.dma_start(bias_f[:], b_f)
-        nc.scalar.dma_start(pre_f[:], xf)
-
         child_w = [held.tile([C, PIECE], F32, name=f"child_w{k}") for k in range(PIECES)]
+        bias_o = held.tile([C, 1], F32, name="bias_o")
+        pre_o = held.tile([C, S], F32, name="pre_o")
         for k in range(PIECES):
             row = cw[:, k * PIECE : (k + 1) * PIECE].rearrange("o n -> (o n)")
             nc.sync.dma_start(child_w[k][:], row.partition_broadcast(C))
-
-        bias_o = held.tile([C, 1], F32, name="bias_o")
-        pre_o = held.tile([C, S], F32, name="pre_o")
-        nc.scalar.dma_start(bias_o[:], b_o)
-        nc.scalar.dma_start(pre_o[:], xo)
+            if k == 0:
+                nc.sync.dma_start(bias_o[:], b_o)
+                nc.sync.dma_start(pre_o[:], xo)
 
         cell = held.tile([C, S], F32, name="cell")
         gate_i = held.tile([C, S], F32, name="gate_i")
@@ -59,14 +67,18 @@ def tile_batchedchildsumtreelstm_kernel(tc, xi, xo, xu, xf, b_i, b_o, b_u, b_f, 
             nc.vector.tensor_tensor(cell[:, columns], gate_i[:, columns], update[:, columns], ALU.mult)
 
         gate_f = held.tile([C, A], F32, name="gate_f")
-        gate_o = held.tile([C, S], F32, name="gate_o")
         nc.scalar.activation(gate_f[:], pre_f[:], ACT.Sigmoid, bias=bias_f[:])
-        nc.scalar.activation(gate_o[:], pre_o[:], ACT.Sigmoid, bias=bias_o[:])
 
-        state = held.tile([C, S], F32, name="state")
+        gate_o = held.tile([C, S], F32, name="gate_o")
         hidden = held.tile([C, S], F32, name="hidden")
+        def finish(k):
+            nodes = slice(k * NODES, (k + 1) * NODES)
+            nc.vector.tensor_tensor(hidden[:, nodes], hidden[:, nodes], gate_o[:, nodes], ALU.mult)
+            nc.sync.dma_start(out[:, nodes], hidden[:, nodes])
+
         for k in range(PIECES):
             nodes = slice(k * NODES, (k + 1) * NODES)
+
             fw = held.tile([C, PIECE], F32, name=f"fw{k}")
             nc.vector.tensor_tensor(
                 fw[:].rearrange("c (t a) -> c t a", a=A),
@@ -74,6 +86,7 @@ def tile_batchedchildsumtreelstm_kernel(tc, xi, xo, xu, xf, b_i, b_o, b_u, b_f, 
                 gate_f[:].unsqueeze(1).to_broadcast([C, NODES, A]),
                 ALU.mult,
             )
+
             product = held.tile([C, PIECE], F32, name=f"product{k}")
             nc.vector.tensor_tensor(
                 product[:],
@@ -81,8 +94,16 @@ def tile_batchedchildsumtreelstm_kernel(tc, xi, xo, xu, xf, b_i, b_o, b_u, b_f, 
                 fw[:],
                 ALU.mult,
             )
-            nc.vector.tensor_reduce(state[:, nodes], product[:].rearrange("c (t a) -> c t a", a=A), AXIS.X, ALU.add)
-            nc.vector.tensor_tensor(state[:, nodes], state[:, nodes], cell[:, nodes], ALU.add)
-            nc.scalar.activation(hidden[:, nodes], state[:, nodes], ACT.Tanh)
-            nc.vector.tensor_tensor(hidden[:, nodes], hidden[:, nodes], gate_o[:, nodes], ALU.mult)
-            nc.sync.dma_start(out[:, nodes], hidden[:, nodes])
+
+            state = sums.tile([C, NODES], F32, name=f"state{k}")
+            nc.tensor.matmul(state[:], identity[:], cell[:, nodes], start=True, stop=False)
+            by_slot = product[:].rearrange("c (t a) -> c a t", a=A)
+            for a in range(A):
+                nc.tensor.matmul(state[:], identity[:], by_slot[:, a, :], start=False, stop=(a == A - 1))
+
+            nc.scalar.activation(gate_o[:, nodes], pre_o[:, nodes], ACT.Sigmoid, bias=bias_o[:])
+            nc.scalar.activation(hidden[:, nodes], state[:], ACT.Tanh)
+            if k >= LAG:
+                finish(k - LAG)
+        for k in range(PIECES - LAG, PIECES):
+            finish(k)

@@ -1,10 +1,10 @@
 import concourse.mybir as mybir
-from concourse.masks import make_identity
 
 F32 = mybir.dt.float32
 U16 = mybir.dt.uint16
 ACT = mybir.ActivationFunctionType
 ALU = mybir.AluOpType
+AXIS = mybir.AxisListType
 
 C = 128
 S = 1024
@@ -15,18 +15,14 @@ PIECES = N // PIECE
 NODES = PIECE // A
 CHUNK = 256
 CHUNKS = S // CHUNK
-LAG = 2
 
 
 def tile_batchedchildsumtreelstm_kernel(tc, xi, xo, xu, xf, b_i, b_o, b_u, b_f, cw, offs, out):
     nc = tc.nc
-    with tc.tile_pool(name="held", bufs=1) as held, tc.psum_pool(name="sums", bufs=1) as sums:
+    with tc.tile_pool(name="held", bufs=1) as held:
         warm = held.tile([C, 1], F32, name="warm")
         nc.vector.memset(warm[:], 0.0)
         nc.scalar.activation(warm[:], warm[:], ACT.Sigmoid)
-
-        identity = held.tile([C, C], F32, name="identity")
-        make_identity(nc, identity[:])
 
         bias_i = held.tile([C, 1], F32, name="bias_i")
         bias_u = held.tile([C, 1], F32, name="bias_u")
@@ -53,7 +49,7 @@ def tile_batchedchildsumtreelstm_kernel(tc, xi, xo, xu, xf, b_i, b_o, b_u, b_f, 
         for k in range(PIECES):
             row = cw[:, k * PIECE : (k + 1) * PIECE].rearrange("o n -> (o n)")
             nc.sync.dma_start(child_w[k][:], row.partition_broadcast(C))
-            if k == 0:
+            if k == 1:
                 nc.sync.dma_start(bias_o[:], b_o)
                 nc.sync.dma_start(pre_o[:], xo)
 
@@ -70,21 +66,18 @@ def tile_batchedchildsumtreelstm_kernel(tc, xi, xo, xu, xf, b_i, b_o, b_u, b_f, 
         nc.scalar.activation(gate_f[:], pre_f[:], ACT.Sigmoid, bias=bias_f[:])
 
         gate_o = held.tile([C, S], F32, name="gate_o")
+        state = held.tile([C, S], F32, name="state")
         hidden = held.tile([C, S], F32, name="hidden")
-        def finish(k):
-            nodes = slice(k * NODES, (k + 1) * NODES)
-            nc.vector.tensor_tensor(hidden[:, nodes], hidden[:, nodes], gate_o[:, nodes], ALU.mult)
-            nc.sync.dma_start(out[:, nodes], hidden[:, nodes])
-
         for k in range(PIECES):
             nodes = slice(k * NODES, (k + 1) * NODES)
 
+            slot_major = held.tile([C, A, NODES], F32, name=f"slot_major{k}")
+            by_slot = child_w[k][:].rearrange("c (t a) -> c a t", a=A)
+            for a in range(A):
+                nc.scalar.activation(slot_major[:, a, :], by_slot[:, a, :], ACT.Copy, scale=gate_f[:, a : a + 1])
             fw = held.tile([C, PIECE], F32, name=f"fw{k}")
-            nc.vector.tensor_tensor(
-                fw[:].rearrange("c (t a) -> c t a", a=A),
-                child_w[k][:].rearrange("c (t a) -> c t a", a=A),
-                gate_f[:].unsqueeze(1).to_broadcast([C, NODES, A]),
-                ALU.mult,
+            nc.scalar.activation(
+                fw[:].rearrange("c (t a) -> c t a", a=A), slot_major[:].rearrange("c a t -> c t a"), ACT.Copy
             )
 
             product = held.tile([C, PIECE], F32, name=f"product{k}")
@@ -95,15 +88,10 @@ def tile_batchedchildsumtreelstm_kernel(tc, xi, xo, xu, xf, b_i, b_o, b_u, b_f, 
                 ALU.mult,
             )
 
-            state = sums.tile([C, NODES], F32, name=f"state{k}")
-            nc.tensor.matmul(state[:], identity[:], cell[:, nodes], start=True, stop=False)
-            by_slot = product[:].rearrange("c (t a) -> c a t", a=A)
-            for a in range(A):
-                nc.tensor.matmul(state[:], identity[:], by_slot[:, a, :], start=False, stop=(a == A - 1))
+            nc.vector.tensor_reduce(state[:, nodes], product[:].rearrange("c (t a) -> c t a", a=A), AXIS.X, ALU.add)
+            nc.vector.tensor_tensor(state[:, nodes], state[:, nodes], cell[:, nodes], ALU.add)
 
             nc.scalar.activation(gate_o[:, nodes], pre_o[:, nodes], ACT.Sigmoid, bias=bias_o[:])
-            nc.scalar.activation(hidden[:, nodes], state[:], ACT.Tanh)
-            if k >= LAG:
-                finish(k - LAG)
-        for k in range(PIECES - LAG, PIECES):
-            finish(k)
+            nc.scalar.activation(hidden[:, nodes], state[:, nodes], ACT.Tanh)
+            nc.vector.tensor_tensor(hidden[:, nodes], hidden[:, nodes], gate_o[:, nodes], ALU.mult)
+            nc.sync.dma_start(out[:, nodes], hidden[:, nodes])

@@ -1,4 +1,5 @@
 import concourse.mybir as mybir
+from concourse.masks import make_identity
 
 F32 = mybir.dt.float32
 U16 = mybir.dt.uint16
@@ -13,16 +14,20 @@ N = S * A
 PIECE = 512
 PIECES = N // PIECE
 NODES = PIECE // A
-CHUNK = 256
+CHUNK = 512
 CHUNKS = S // CHUNK
+LAG = 2
 
 
 def tile_batchedchildsumtreelstm_kernel(tc, xi, xo, xu, xf, b_i, b_o, b_u, b_f, cw, offs, out):
     nc = tc.nc
-    with tc.tile_pool(name="held", bufs=1) as held:
+    with tc.tile_pool(name="held", bufs=1) as held, tc.psum_pool(name="sums", bufs=1) as sums:
         warm = held.tile([C, 1], F32, name="warm")
         nc.vector.memset(warm[:], 0.0)
         nc.scalar.activation(warm[:], warm[:], ACT.Sigmoid)
+
+        identity = held.tile([C, C], F32, name="identity")
+        make_identity(nc, identity[:])
 
         bias_i = held.tile([C, 1], F32, name="bias_i")
         bias_u = held.tile([C, 1], F32, name="bias_u")
@@ -66,11 +71,19 @@ def tile_batchedchildsumtreelstm_kernel(tc, xi, xo, xu, xf, b_i, b_o, b_u, b_f, 
         nc.scalar.activation(gate_f[:], pre_f[:], ACT.Sigmoid, bias=bias_f[:])
 
         gate_o = held.tile([C, S], F32, name="gate_o")
-        state = held.tile([C, S], F32, name="state")
         hidden = held.tile([C, S], F32, name="hidden")
-        for k in range(PIECES):
-            nodes = slice(k * NODES, (k + 1) * NODES)
 
+        def fw_on_vector(k):
+            fw = held.tile([C, PIECE], F32, name=f"fw{k}")
+            nc.vector.tensor_tensor(
+                fw[:].rearrange("c (t a) -> c t a", a=A),
+                child_w[k][:].rearrange("c (t a) -> c t a", a=A),
+                gate_f[:].unsqueeze(1).to_broadcast([C, NODES, A]),
+                ALU.mult,
+            )
+            return fw
+
+        def fw_on_scalar(k):
             slot_major = held.tile([C, A, NODES], F32, name=f"slot_major{k}")
             by_slot = child_w[k][:].rearrange("c (t a) -> c a t", a=A)
             for a in range(A):
@@ -79,6 +92,30 @@ def tile_batchedchildsumtreelstm_kernel(tc, xi, xo, xu, xf, b_i, b_o, b_u, b_f, 
             nc.scalar.activation(
                 fw[:].rearrange("c (t a) -> c t a", a=A), slot_major[:].rearrange("c a t -> c t a"), ACT.Copy
             )
+            return fw
+
+        def sum_on_tensor(k, product):
+            state = sums.tile([C, NODES], F32, name=f"state{k}")
+            nc.tensor.matmul(state[:], identity[:], cell[:, k * NODES : (k + 1) * NODES], start=True, stop=False)
+            by_slot = product[:].rearrange("c (t a) -> c a t", a=A)
+            for a in range(A):
+                nc.tensor.matmul(state[:], identity[:], by_slot[:, a, :], start=False, stop=(a == A - 1))
+            return state
+
+        def sum_on_vector(k, product):
+            state = held.tile([C, NODES], F32, name=f"state{k}")
+            nc.vector.tensor_reduce(state[:], product[:].rearrange("c (t a) -> c t a", a=A), AXIS.X, ALU.add)
+            nc.vector.tensor_tensor(state[:], state[:], cell[:, k * NODES : (k + 1) * NODES], ALU.add)
+            return state
+
+        def finish(k):
+            nodes = slice(k * NODES, (k + 1) * NODES)
+            nc.vector.tensor_tensor(hidden[:, nodes], hidden[:, nodes], gate_o[:, nodes], ALU.mult)
+            nc.sync.dma_start(out[:, nodes], hidden[:, nodes])
+
+        for k in range(PIECES):
+            nodes = slice(k * NODES, (k + 1) * NODES)
+            fw = fw_on_vector(k) if k % 2 == 0 else fw_on_scalar(k)
 
             product = held.tile([C, PIECE], F32, name=f"product{k}")
             nc.vector.tensor_tensor(
@@ -88,10 +125,10 @@ def tile_batchedchildsumtreelstm_kernel(tc, xi, xo, xu, xf, b_i, b_o, b_u, b_f, 
                 ALU.mult,
             )
 
-            nc.vector.tensor_reduce(state[:, nodes], product[:].rearrange("c (t a) -> c t a", a=A), AXIS.X, ALU.add)
-            nc.vector.tensor_tensor(state[:, nodes], state[:, nodes], cell[:, nodes], ALU.add)
-
+            state = sum_on_tensor(k, product) if k % 2 == 0 else sum_on_vector(k, product)
             nc.scalar.activation(gate_o[:, nodes], pre_o[:, nodes], ACT.Sigmoid, bias=bias_o[:])
-            nc.scalar.activation(hidden[:, nodes], state[:, nodes], ACT.Tanh)
-            nc.vector.tensor_tensor(hidden[:, nodes], hidden[:, nodes], gate_o[:, nodes], ALU.mult)
-            nc.sync.dma_start(out[:, nodes], hidden[:, nodes])
+            nc.scalar.activation(hidden[:, nodes], state[:], ACT.Tanh)
+            if k >= LAG:
+                finish(k - LAG)
+        for k in range(PIECES - LAG, PIECES):
+            finish(k)

@@ -16,6 +16,7 @@ PIECES = N // PIECE
 NODES = PIECE // A
 CHUNK = 512
 CHUNKS = S // CHUNK
+CW_PIECE = 1024
 LAG = 2
 
 
@@ -28,6 +29,11 @@ def tile_batchedchildsumtreelstm_kernel(tc, xi, xo, xu, xf, b_i, b_o, b_u, b_f, 
 
         identity = held.tile([C, C], F32, name="identity")
         make_identity(nc, identity[:])
+
+        child_w = held.tile([C, N], F32, name="child_w")
+        for m in range(N // CW_PIECE):
+            entries = slice(m * CW_PIECE, (m + 1) * CW_PIECE)
+            nc.gpsimd.dma_start(child_w[:, entries], cw[:, entries].rearrange("o n -> (o n)").partition_broadcast(C))
 
         bias_i = held.tile([C, 1], F32, name="bias_i")
         bias_u = held.tile([C, 1], F32, name="bias_u")
@@ -48,15 +54,10 @@ def tile_batchedchildsumtreelstm_kernel(tc, xi, xo, xu, xf, b_i, b_o, b_u, b_f, 
         offsets = held.tile([C, N // 16], U16, name="offsets")
         nc.sync.dma_start(offsets[:], offs)
 
-        child_w = [held.tile([C, PIECE], F32, name=f"child_w{k}") for k in range(PIECES)]
         bias_o = held.tile([C, 1], F32, name="bias_o")
         pre_o = held.tile([C, S], F32, name="pre_o")
-        for k in range(PIECES):
-            row = cw[:, k * PIECE : (k + 1) * PIECE].rearrange("o n -> (o n)")
-            nc.sync.dma_start(child_w[k][:], row.partition_broadcast(C))
-            if k == 1:
-                nc.sync.dma_start(bias_o[:], b_o)
-                nc.sync.dma_start(pre_o[:], xo)
+        nc.sync.dma_start(bias_o[:], b_o)
+        nc.sync.dma_start(pre_o[:], xo)
 
         cell = held.tile([C, S], F32, name="cell")
         gate_i = held.tile([C, S], F32, name="gate_i")
@@ -77,7 +78,7 @@ def tile_batchedchildsumtreelstm_kernel(tc, xi, xo, xu, xf, b_i, b_o, b_u, b_f, 
             fw = held.tile([C, PIECE], F32, name=f"fw{k}")
             nc.vector.tensor_tensor(
                 fw[:].rearrange("c (t a) -> c t a", a=A),
-                child_w[k][:].rearrange("c (t a) -> c t a", a=A),
+                child_w[:, k * PIECE : (k + 1) * PIECE].rearrange("c (t a) -> c t a", a=A),
                 gate_f[:].unsqueeze(1).to_broadcast([C, NODES, A]),
                 ALU.mult,
             )
@@ -85,7 +86,7 @@ def tile_batchedchildsumtreelstm_kernel(tc, xi, xo, xu, xf, b_i, b_o, b_u, b_f, 
 
         def fw_on_scalar(k):
             slot_major = held.tile([C, A, NODES], F32, name=f"slot_major{k}")
-            by_slot = child_w[k][:].rearrange("c (t a) -> c a t", a=A)
+            by_slot = child_w[:, k * PIECE : (k + 1) * PIECE].rearrange("c (t a) -> c a t", a=A)
             for a in range(A):
                 nc.scalar.activation(slot_major[:, a, :], by_slot[:, a, :], ACT.Copy, scale=gate_f[:, a : a + 1])
             fw = held.tile([C, PIECE], F32, name=f"fw{k}")

@@ -11,13 +11,12 @@ C = 128
 S = 1024
 A = 4
 N = S * A
-PIECE = 512
+PIECE = S
 PIECES = N // PIECE
 NODES = PIECE // A
-CHUNK = 512
-CHUNKS = S // CHUNK
-CW_PIECE = 1024
-LAG = 2
+HALF = S // 2
+VECTOR_FW = 2
+TENSOR_SUMS = 3
 
 
 def tile_batchedchildsumtreelstm_kernel(tc, xi, xo, xu, xf, b_i, b_o, b_u, b_f, cw, offs, out):
@@ -30,21 +29,24 @@ def tile_batchedchildsumtreelstm_kernel(tc, xi, xo, xu, xf, b_i, b_o, b_u, b_f, 
         identity = held.tile([C, C], F32, name="identity")
         make_identity(nc, identity[:])
 
-        child_w = held.tile([C, N], F32, name="child_w")
-        for m in range(N // CW_PIECE):
-            entries = slice(m * CW_PIECE, (m + 1) * CW_PIECE)
-            nc.gpsimd.dma_start(child_w[:, entries], cw[:, entries].rearrange("o n -> (o n)").partition_broadcast(C))
+        child_w = [held.tile([C, PIECE], F32, name=f"child_w{k}") for k in range(PIECES)]
+
+        def load_child_w(queue, k):
+            row = cw[:, k * PIECE : (k + 1) * PIECE].rearrange("o n -> (o n)")
+            queue.dma_start(child_w[k][:], row.partition_broadcast(C))
+
+        for k in range(VECTOR_FW):
+            load_child_w(nc.gpsimd, k)
 
         bias_i = held.tile([C, 1], F32, name="bias_i")
         bias_u = held.tile([C, 1], F32, name="bias_u")
         nc.sync.dma_start(bias_i[:], b_i)
         nc.sync.dma_start(bias_u[:], b_u)
-        pre_i = [held.tile([C, CHUNK], F32, name=f"pre_i{h}") for h in range(CHUNKS)]
-        pre_u = [held.tile([C, CHUNK], F32, name=f"pre_u{h}") for h in range(CHUNKS)]
-        for h in range(CHUNKS):
-            columns = slice(h * CHUNK, (h + 1) * CHUNK)
-            nc.sync.dma_start(pre_i[h][:], xi[:, columns])
-            nc.sync.dma_start(pre_u[h][:], xu[:, columns])
+        pre_i = held.tile([C, S], F32, name="pre_i")
+        pre_u = held.tile([C, S], F32, name="pre_u")
+        for columns in (slice(0, HALF), slice(HALF, S)):
+            nc.sync.dma_start(pre_i[:, columns], xi[:, columns])
+            nc.sync.dma_start(pre_u[:, columns], xu[:, columns])
 
         bias_f = held.tile([C, 1], F32, name="bias_f")
         pre_f = held.tile([C, A], F32, name="pre_f")
@@ -54,6 +56,9 @@ def tile_batchedchildsumtreelstm_kernel(tc, xi, xo, xu, xf, b_i, b_o, b_u, b_f, 
         offsets = held.tile([C, N // 16], U16, name="offsets")
         nc.sync.dma_start(offsets[:], offs)
 
+        for k in range(VECTOR_FW, PIECES):
+            load_child_w(nc.sync, k)
+
         bias_o = held.tile([C, 1], F32, name="bias_o")
         pre_o = held.tile([C, S], F32, name="pre_o")
         nc.sync.dma_start(bias_o[:], b_o)
@@ -62,23 +67,19 @@ def tile_batchedchildsumtreelstm_kernel(tc, xi, xo, xu, xf, b_i, b_o, b_u, b_f, 
         cell = held.tile([C, S], F32, name="cell")
         gate_i = held.tile([C, S], F32, name="gate_i")
         update = held.tile([C, S], F32, name="update")
-        for h in range(CHUNKS):
-            columns = slice(h * CHUNK, (h + 1) * CHUNK)
-            nc.scalar.activation(gate_i[:, columns], pre_i[h][:], ACT.Sigmoid, bias=bias_i[:])
-            nc.scalar.activation(update[:, columns], pre_u[h][:], ACT.Tanh, bias=bias_u[:])
+        for columns in (slice(0, HALF), slice(HALF, S)):
+            nc.scalar.activation(gate_i[:, columns], pre_i[:, columns], ACT.Sigmoid, bias=bias_i[:])
+            nc.scalar.activation(update[:, columns], pre_u[:, columns], ACT.Tanh, bias=bias_u[:])
             nc.vector.tensor_tensor(cell[:, columns], gate_i[:, columns], update[:, columns], ALU.mult)
 
         gate_f = held.tile([C, A], F32, name="gate_f")
         nc.scalar.activation(gate_f[:], pre_f[:], ACT.Sigmoid, bias=bias_f[:])
 
-        gate_o = held.tile([C, S], F32, name="gate_o")
-        hidden = held.tile([C, S], F32, name="hidden")
-
         def fw_on_vector(k):
             fw = held.tile([C, PIECE], F32, name=f"fw{k}")
             nc.vector.tensor_tensor(
                 fw[:].rearrange("c (t a) -> c t a", a=A),
-                child_w[:, k * PIECE : (k + 1) * PIECE].rearrange("c (t a) -> c t a", a=A),
+                child_w[k][:].rearrange("c (t a) -> c t a", a=A),
                 gate_f[:].unsqueeze(1).to_broadcast([C, NODES, A]),
                 ALU.mult,
             )
@@ -86,7 +87,7 @@ def tile_batchedchildsumtreelstm_kernel(tc, xi, xo, xu, xf, b_i, b_o, b_u, b_f, 
 
         def fw_on_scalar(k):
             slot_major = held.tile([C, A, NODES], F32, name=f"slot_major{k}")
-            by_slot = child_w[:, k * PIECE : (k + 1) * PIECE].rearrange("c (t a) -> c a t", a=A)
+            by_slot = child_w[k][:].rearrange("c (t a) -> c a t", a=A)
             for a in range(A):
                 nc.scalar.activation(slot_major[:, a, :], by_slot[:, a, :], ACT.Copy, scale=gate_f[:, a : a + 1])
             fw = held.tile([C, PIECE], F32, name=f"fw{k}")
@@ -109,14 +110,14 @@ def tile_batchedchildsumtreelstm_kernel(tc, xi, xo, xu, xf, b_i, b_o, b_u, b_f, 
             nc.vector.tensor_tensor(state[:], state[:], cell[:, k * NODES : (k + 1) * NODES], ALU.add)
             return state
 
-        def finish(k):
-            nodes = slice(k * NODES, (k + 1) * NODES)
-            nc.vector.tensor_tensor(hidden[:, nodes], hidden[:, nodes], gate_o[:, nodes], ALU.mult)
-            nc.sync.dma_start(out[:, nodes], hidden[:, nodes])
+        fw_from_scalar = {k: fw_on_scalar(k) for k in range(VECTOR_FW, PIECES)}
 
+        gate_o = held.tile([C, S], F32, name="gate_o")
+        nc.scalar.activation(gate_o[:], pre_o[:], ACT.Sigmoid, bias=bias_o[:])
+
+        states = []
         for k in range(PIECES):
-            nodes = slice(k * NODES, (k + 1) * NODES)
-            fw = fw_on_vector(k) if k % 2 == 0 else fw_on_scalar(k)
+            fw = fw_on_vector(k) if k < VECTOR_FW else fw_from_scalar[k]
 
             product = held.tile([C, PIECE], F32, name=f"product{k}")
             nc.vector.tensor_tensor(
@@ -125,11 +126,11 @@ def tile_batchedchildsumtreelstm_kernel(tc, xi, xo, xu, xf, b_i, b_o, b_u, b_f, 
                 fw[:],
                 ALU.mult,
             )
+            states.append(sum_on_tensor(k, product) if k < TENSOR_SUMS else sum_on_vector(k, product))
 
-            state = sum_on_tensor(k, product) if k % 2 == 0 else sum_on_vector(k, product)
-            nc.scalar.activation(gate_o[:, nodes], pre_o[:, nodes], ACT.Sigmoid, bias=bias_o[:])
-            nc.scalar.activation(hidden[:, nodes], state[:], ACT.Tanh)
-            if k >= LAG:
-                finish(k - LAG)
-        for k in range(PIECES - LAG, PIECES):
-            finish(k)
+        hidden = held.tile([C, S], F32, name="hidden")
+        for k in range(PIECES):
+            nodes = slice(k * NODES, (k + 1) * NODES)
+            nc.scalar.activation(hidden[:, nodes], states[k][:], ACT.Tanh)
+            nc.vector.tensor_tensor(hidden[:, nodes], hidden[:, nodes], gate_o[:, nodes], ALU.mult)
+            nc.sync.dma_start(out[:, nodes], hidden[:, nodes])

@@ -11,12 +11,14 @@ C = 128
 S = 1024
 A = 4
 N = S * A
-PIECE = S
+PIECE = 512
 PIECES = N // PIECE
 NODES = PIECE // A
-HALF = S // 2
-VECTOR_FW = 2
-TENSOR_SUMS = 3
+CHUNK = 512
+CHUNKS = S // CHUNK
+CW_LOADS = (1024, 1024, 1024, 512, 512)
+assert sum(CW_LOADS) == N
+LAG = 2
 
 
 def tile_batchedchildsumtreelstm_kernel(tc, xi, xo, xu, xf, b_i, b_o, b_u, b_f, cw, offs, out):
@@ -26,27 +28,26 @@ def tile_batchedchildsumtreelstm_kernel(tc, xi, xo, xu, xf, b_i, b_o, b_u, b_f, 
         nc.vector.memset(warm[:], 0.0)
         nc.scalar.activation(warm[:], warm[:], ACT.Sigmoid)
 
+        child_w = held.tile([C, N], F32, name="child_w")
+        first = 0
+        for entries_loaded in CW_LOADS:
+            entries = slice(first, first + entries_loaded)
+            nc.gpsimd.dma_start(child_w[:, entries], cw[:, entries].rearrange("o n -> (o n)").partition_broadcast(C))
+            first += entries_loaded
+
         identity = held.tile([C, C], F32, name="identity")
         make_identity(nc, identity[:])
-
-        child_w = [held.tile([C, PIECE], F32, name=f"child_w{k}") for k in range(PIECES)]
-
-        def load_child_w(queue, k):
-            row = cw[:, k * PIECE : (k + 1) * PIECE].rearrange("o n -> (o n)")
-            queue.dma_start(child_w[k][:], row.partition_broadcast(C))
-
-        for k in range(VECTOR_FW):
-            load_child_w(nc.gpsimd, k)
 
         bias_i = held.tile([C, 1], F32, name="bias_i")
         bias_u = held.tile([C, 1], F32, name="bias_u")
         nc.sync.dma_start(bias_i[:], b_i)
         nc.sync.dma_start(bias_u[:], b_u)
-        pre_i = held.tile([C, S], F32, name="pre_i")
-        pre_u = held.tile([C, S], F32, name="pre_u")
-        for columns in (slice(0, HALF), slice(HALF, S)):
-            nc.sync.dma_start(pre_i[:, columns], xi[:, columns])
-            nc.sync.dma_start(pre_u[:, columns], xu[:, columns])
+        pre_i = [held.tile([C, CHUNK], F32, name=f"pre_i{h}") for h in range(CHUNKS)]
+        pre_u = [held.tile([C, CHUNK], F32, name=f"pre_u{h}") for h in range(CHUNKS)]
+        for h in range(CHUNKS):
+            columns = slice(h * CHUNK, (h + 1) * CHUNK)
+            nc.sync.dma_start(pre_i[h][:], xi[:, columns])
+            nc.sync.dma_start(pre_u[h][:], xu[:, columns])
 
         bias_f = held.tile([C, 1], F32, name="bias_f")
         pre_f = held.tile([C, A], F32, name="pre_f")
@@ -56,9 +57,6 @@ def tile_batchedchildsumtreelstm_kernel(tc, xi, xo, xu, xf, b_i, b_o, b_u, b_f, 
         offsets = held.tile([C, N // 16], U16, name="offsets")
         nc.sync.dma_start(offsets[:], offs)
 
-        for k in range(VECTOR_FW, PIECES):
-            load_child_w(nc.sync, k)
-
         bias_o = held.tile([C, 1], F32, name="bias_o")
         pre_o = held.tile([C, S], F32, name="pre_o")
         nc.sync.dma_start(bias_o[:], b_o)
@@ -67,19 +65,23 @@ def tile_batchedchildsumtreelstm_kernel(tc, xi, xo, xu, xf, b_i, b_o, b_u, b_f, 
         cell = held.tile([C, S], F32, name="cell")
         gate_i = held.tile([C, S], F32, name="gate_i")
         update = held.tile([C, S], F32, name="update")
-        for columns in (slice(0, HALF), slice(HALF, S)):
-            nc.scalar.activation(gate_i[:, columns], pre_i[:, columns], ACT.Sigmoid, bias=bias_i[:])
-            nc.scalar.activation(update[:, columns], pre_u[:, columns], ACT.Tanh, bias=bias_u[:])
+        for h in range(CHUNKS):
+            columns = slice(h * CHUNK, (h + 1) * CHUNK)
+            nc.scalar.activation(gate_i[:, columns], pre_i[h][:], ACT.Sigmoid, bias=bias_i[:])
+            nc.scalar.activation(update[:, columns], pre_u[h][:], ACT.Tanh, bias=bias_u[:])
             nc.vector.tensor_tensor(cell[:, columns], gate_i[:, columns], update[:, columns], ALU.mult)
 
         gate_f = held.tile([C, A], F32, name="gate_f")
         nc.scalar.activation(gate_f[:], pre_f[:], ACT.Sigmoid, bias=bias_f[:])
 
+        gate_o = held.tile([C, S], F32, name="gate_o")
+        hidden = held.tile([C, S], F32, name="hidden")
+
         def fw_on_vector(k):
             fw = held.tile([C, PIECE], F32, name=f"fw{k}")
             nc.vector.tensor_tensor(
                 fw[:].rearrange("c (t a) -> c t a", a=A),
-                child_w[k][:].rearrange("c (t a) -> c t a", a=A),
+                child_w[:, k * PIECE : (k + 1) * PIECE].rearrange("c (t a) -> c t a", a=A),
                 gate_f[:].unsqueeze(1).to_broadcast([C, NODES, A]),
                 ALU.mult,
             )
@@ -87,7 +89,7 @@ def tile_batchedchildsumtreelstm_kernel(tc, xi, xo, xu, xf, b_i, b_o, b_u, b_f, 
 
         def fw_on_scalar(k):
             slot_major = held.tile([C, A, NODES], F32, name=f"slot_major{k}")
-            by_slot = child_w[k][:].rearrange("c (t a) -> c a t", a=A)
+            by_slot = child_w[:, k * PIECE : (k + 1) * PIECE].rearrange("c (t a) -> c a t", a=A)
             for a in range(A):
                 nc.scalar.activation(slot_major[:, a, :], by_slot[:, a, :], ACT.Copy, scale=gate_f[:, a : a + 1])
             fw = held.tile([C, PIECE], F32, name=f"fw{k}")
@@ -110,14 +112,14 @@ def tile_batchedchildsumtreelstm_kernel(tc, xi, xo, xu, xf, b_i, b_o, b_u, b_f, 
             nc.vector.tensor_tensor(state[:], state[:], cell[:, k * NODES : (k + 1) * NODES], ALU.add)
             return state
 
-        fw_from_scalar = {k: fw_on_scalar(k) for k in range(VECTOR_FW, PIECES)}
+        def finish(k):
+            nodes = slice(k * NODES, (k + 1) * NODES)
+            nc.vector.tensor_tensor(hidden[:, nodes], hidden[:, nodes], gate_o[:, nodes], ALU.mult)
+            nc.sync.dma_start(out[:, nodes], hidden[:, nodes])
 
-        gate_o = held.tile([C, S], F32, name="gate_o")
-        nc.scalar.activation(gate_o[:], pre_o[:], ACT.Sigmoid, bias=bias_o[:])
-
-        states = []
         for k in range(PIECES):
-            fw = fw_on_vector(k) if k < VECTOR_FW else fw_from_scalar[k]
+            nodes = slice(k * NODES, (k + 1) * NODES)
+            fw = fw_on_scalar(k) if k % 2 == 0 else fw_on_vector(k)
 
             product = held.tile([C, PIECE], F32, name=f"product{k}")
             nc.vector.tensor_tensor(
@@ -126,11 +128,11 @@ def tile_batchedchildsumtreelstm_kernel(tc, xi, xo, xu, xf, b_i, b_o, b_u, b_f, 
                 fw[:],
                 ALU.mult,
             )
-            states.append(sum_on_tensor(k, product) if k < TENSOR_SUMS else sum_on_vector(k, product))
 
-        hidden = held.tile([C, S], F32, name="hidden")
-        for k in range(PIECES):
-            nodes = slice(k * NODES, (k + 1) * NODES)
-            nc.scalar.activation(hidden[:, nodes], states[k][:], ACT.Tanh)
-            nc.vector.tensor_tensor(hidden[:, nodes], hidden[:, nodes], gate_o[:, nodes], ALU.mult)
-            nc.sync.dma_start(out[:, nodes], hidden[:, nodes])
+            state = sum_on_tensor(k, product) if k % 2 == 0 else sum_on_vector(k, product)
+            nc.scalar.activation(gate_o[:, nodes], pre_o[:, nodes], ACT.Sigmoid, bias=bias_o[:])
+            nc.scalar.activation(hidden[:, nodes], state[:], ACT.Tanh)
+            if k >= LAG:
+                finish(k - LAG)
+        for k in range(PIECES - LAG, PIECES):
+            finish(k)

@@ -16,9 +16,13 @@ PIECES = N // PIECE
 NODES = PIECE // A
 CHUNK = 512
 CHUNKS = S // CHUNK
-CW_LOADS = (1024, 1024, 1024, 512, 512)
+CW_LOADS = (512, 512, 1024, 1024, 1024)
 assert sum(CW_LOADS) == N
-LAG = 2
+FW_VECTOR_EVERY = 4
+FW_AHEAD = 4
+TANH_LAG = 2
+LAG = 4
+HALF = S // 2
 
 
 def tile_batchedchildsumtreelstm_kernel(tc, xi, xo, xu, xf, b_i, b_o, b_u, b_f, cw, offs, out):
@@ -28,23 +32,18 @@ def tile_batchedchildsumtreelstm_kernel(tc, xi, xo, xu, xf, b_i, b_o, b_u, b_f, 
         nc.vector.memset(warm[:], 0.0)
         nc.scalar.activation(warm[:], warm[:], ACT.Sigmoid)
 
-        child_w = held.tile([C, N], F32, name="child_w")
-        first = 0
-        for entries_loaded in CW_LOADS:
-            entries = slice(first, first + entries_loaded)
-            nc.gpsimd.dma_start(child_w[:, entries], cw[:, entries].rearrange("o n -> (o n)").partition_broadcast(C))
-            first += entries_loaded
-
         identity = held.tile([C, C], F32, name="identity")
         make_identity(nc, identity[:])
 
         bias_i = held.tile([C, 1], F32, name="bias_i")
         bias_u = held.tile([C, 1], F32, name="bias_u")
-        nc.sync.dma_start(bias_i[:], b_i)
-        nc.sync.dma_start(bias_u[:], b_u)
         pre_i = [held.tile([C, CHUNK], F32, name=f"pre_i{h}") for h in range(CHUNKS)]
         pre_u = [held.tile([C, CHUNK], F32, name=f"pre_u{h}") for h in range(CHUNKS)]
-        for h in range(CHUNKS):
+        nc.sync.dma_start(bias_i[:], b_i)
+        nc.sync.dma_start(pre_i[0][:], xi[:, 0:CHUNK])
+        nc.sync.dma_start(bias_u[:], b_u)
+        nc.sync.dma_start(pre_u[0][:], xu[:, 0:CHUNK])
+        for h in range(1, CHUNKS):
             columns = slice(h * CHUNK, (h + 1) * CHUNK)
             nc.sync.dma_start(pre_i[h][:], xi[:, columns])
             nc.sync.dma_start(pre_u[h][:], xu[:, columns])
@@ -54,28 +53,30 @@ def tile_batchedchildsumtreelstm_kernel(tc, xi, xo, xu, xf, b_i, b_o, b_u, b_f, 
         nc.sync.dma_start(bias_f[:], b_f)
         nc.sync.dma_start(pre_f[:], xf)
 
+        child_w = held.tile([C, N], F32, name="child_w")
+
+        def load_cw(first, entries_loaded):
+            entries = slice(first, first + entries_loaded)
+            nc.sync.dma_start(child_w[:, entries], cw[:, entries].rearrange("o n -> (o n)").partition_broadcast(C))
+
+        load_cw(CW_LOADS[0], CW_LOADS[1])
+        load_cw(0, CW_LOADS[0])
+
         offsets = held.tile([C, N // 16], U16, name="offsets")
         nc.sync.dma_start(offsets[:], offs)
+
+        load_cw(sum(CW_LOADS[:2]), CW_LOADS[2])
 
         bias_o = held.tile([C, 1], F32, name="bias_o")
         pre_o = held.tile([C, S], F32, name="pre_o")
         nc.sync.dma_start(bias_o[:], b_o)
-        nc.sync.dma_start(pre_o[:], xo)
+        nc.sync.dma_start(pre_o[:, 0:HALF], xo[:, 0:HALF])
 
-        cell = held.tile([C, S], F32, name="cell")
-        gate_i = held.tile([C, S], F32, name="gate_i")
-        update = held.tile([C, S], F32, name="update")
-        for h in range(CHUNKS):
-            columns = slice(h * CHUNK, (h + 1) * CHUNK)
-            nc.scalar.activation(gate_i[:, columns], pre_i[h][:], ACT.Sigmoid, bias=bias_i[:])
-            nc.scalar.activation(update[:, columns], pre_u[h][:], ACT.Tanh, bias=bias_u[:])
-            nc.vector.tensor_tensor(cell[:, columns], gate_i[:, columns], update[:, columns], ALU.mult)
+        load_cw(sum(CW_LOADS[:3]), CW_LOADS[3])
+        load_cw(sum(CW_LOADS[:4]), CW_LOADS[4])
+        nc.sync.dma_start(pre_o[:, HALF:S], xo[:, HALF:S])
 
         gate_f = held.tile([C, A], F32, name="gate_f")
-        nc.scalar.activation(gate_f[:], pre_f[:], ACT.Sigmoid, bias=bias_f[:])
-
-        gate_o = held.tile([C, S], F32, name="gate_o")
-        hidden = held.tile([C, S], F32, name="hidden")
 
         def fw_on_vector(k):
             fw = held.tile([C, PIECE], F32, name=f"fw{k}")
@@ -98,13 +99,32 @@ def tile_batchedchildsumtreelstm_kernel(tc, xi, xo, xu, xf, b_i, b_o, b_u, b_f, 
             )
             return fw
 
-        def sum_on_tensor(k, product):
+        cell = held.tile([C, S], F32, name="cell")
+        gate_i = held.tile([C, S], F32, name="gate_i")
+        update = held.tile([C, S], F32, name="update")
+        for h in range(CHUNKS):
+            columns = slice(h * CHUNK, (h + 1) * CHUNK)
+            nc.scalar.activation(gate_i[:, columns], pre_i[h][:], ACT.Sigmoid, bias=bias_i[:])
+            nc.scalar.activation(update[:, columns], pre_u[h][:], ACT.Tanh, bias=bias_u[:])
+            nc.vector.tensor_tensor(cell[:, columns], gate_i[:, columns], update[:, columns], ALU.mult)
+
+        nc.scalar.activation(gate_f[:], pre_f[:], ACT.Sigmoid, bias=bias_f[:])
+        fws = {k: fw_on_scalar(k) for k in range(FW_AHEAD) if k % FW_VECTOR_EVERY != 0}
+
+        gate_o = held.tile([C, S], F32, name="gate_o")
+        hidden = held.tile([C, S], F32, name="hidden")
+
+        states = []
+        for k in range(PIECES - 1):
             state = sums.tile([C, NODES], F32, name=f"state{k}")
             nc.tensor.matmul(state[:], identity[:], cell[:, k * NODES : (k + 1) * NODES], start=True, stop=False)
+            states.append(state)
+
+        def sum_on_tensor(k, product):
             by_slot = product[:].rearrange("c (t a) -> c a t", a=A)
             for a in range(A):
-                nc.tensor.matmul(state[:], identity[:], by_slot[:, a, :], start=False, stop=(a == A - 1))
-            return state
+                nc.tensor.matmul(states[k][:], identity[:], by_slot[:, a, :], start=False, stop=(a == A - 1))
+            return states[k]
 
         def sum_on_vector(k, product):
             state = held.tile([C, NODES], F32, name=f"state{k}")
@@ -112,27 +132,35 @@ def tile_batchedchildsumtreelstm_kernel(tc, xi, xo, xu, xf, b_i, b_o, b_u, b_f, 
             nc.vector.tensor_tensor(state[:], state[:], cell[:, k * NODES : (k + 1) * NODES], ALU.add)
             return state
 
+        def squash(k):
+            nodes = slice(k * NODES, (k + 1) * NODES)
+            if (k * NODES) % HALF == 0:
+                half = slice(k * NODES, k * NODES + HALF)
+                nc.scalar.activation(gate_o[:, half], pre_o[:, half], ACT.Sigmoid, bias=bias_o[:])
+            nc.scalar.activation(hidden[:, nodes], summed[k][:], ACT.Tanh)
+
         def finish(k):
             nodes = slice(k * NODES, (k + 1) * NODES)
             nc.vector.tensor_tensor(hidden[:, nodes], hidden[:, nodes], gate_o[:, nodes], ALU.mult)
             nc.sync.dma_start(out[:, nodes], hidden[:, nodes])
 
-        for k in range(PIECES):
-            nodes = slice(k * NODES, (k + 1) * NODES)
-            fw = fw_on_scalar(k) if k % 2 == 0 else fw_on_vector(k)
-
-            product = held.tile([C, PIECE], F32, name=f"product{k}")
-            nc.vector.tensor_tensor(
-                product[:],
-                cell[:].indirect(offsets[:, k * (PIECE // 16) : (k + 1) * (PIECE // 16)]),
-                fw[:],
-                ALU.mult,
-            )
-
-            state = sum_on_tensor(k, product) if k % 2 == 0 else sum_on_vector(k, product)
-            nc.scalar.activation(gate_o[:, nodes], pre_o[:, nodes], ACT.Sigmoid, bias=bias_o[:])
-            nc.scalar.activation(hidden[:, nodes], state[:], ACT.Tanh)
+        summed = []
+        for k in range(PIECES + LAG):
+            ahead = k + FW_AHEAD
+            if ahead < PIECES and ahead % FW_VECTOR_EVERY != 0:
+                fws[ahead] = fw_on_scalar(ahead)
+            if k < PIECES:
+                if k % FW_VECTOR_EVERY == 0:
+                    fws[k] = fw_on_vector(k)
+                product = held.tile([C, PIECE], F32, name=f"product{k}")
+                nc.vector.tensor_tensor(
+                    product[:],
+                    cell[:].indirect(offsets[:, k * (PIECE // 16) : (k + 1) * (PIECE // 16)]),
+                    fws[k][:],
+                    ALU.mult,
+                )
+                summed.append(sum_on_tensor(k, product) if k < PIECES - 1 else sum_on_vector(k, product))
+            if TANH_LAG <= k < PIECES + TANH_LAG:
+                squash(k - TANH_LAG)
             if k >= LAG:
                 finish(k - LAG)
-        for k in range(PIECES - LAG, PIECES):
-            finish(k)

@@ -14,14 +14,9 @@ N = S * A
 PIECE = 512
 PIECES = N // PIECE
 NODES = PIECE // A
+EARLY = PIECES // 2
 CHUNK = 512
 CHUNKS = S // CHUNK
-CW_LOADS = (512, 512, 1024, 1024, 1024)
-assert sum(CW_LOADS) == N
-FW_VECTOR_EVERY = 4
-FW_AHEAD = 4
-TANH_LAG = 2
-LAG = 4
 HALF = S // 2
 
 
@@ -54,50 +49,18 @@ def tile_batchedchildsumtreelstm_kernel(tc, xi, xo, xu, xf, b_i, b_o, b_u, b_f, 
         nc.sync.dma_start(pre_f[:], xf)
 
         child_w = held.tile([C, N], F32, name="child_w")
-
-        def load_cw(first, entries_loaded):
-            entries = slice(first, first + entries_loaded)
-            nc.sync.dma_start(child_w[:, entries], cw[:, entries].rearrange("o n -> (o n)").partition_broadcast(C))
-
-        load_cw(CW_LOADS[0], CW_LOADS[1])
-        load_cw(0, CW_LOADS[0])
-
         offsets = held.tile([C, N // 16], U16, name="offsets")
-        nc.sync.dma_start(offsets[:], offs)
-
-        load_cw(sum(CW_LOADS[:2]), CW_LOADS[2])
+        for k in range(EARLY):
+            for piece in (k, EARLY + k):
+                entries = slice(piece * PIECE, (piece + 1) * PIECE)
+                nc.sync.dma_start(child_w[:, entries], cw[:, entries].rearrange("o n -> (o n)").partition_broadcast(C))
+            if k == 0:
+                nc.sync.dma_start(offsets[:], offs)
 
         bias_o = held.tile([C, 1], F32, name="bias_o")
         pre_o = held.tile([C, S], F32, name="pre_o")
         nc.sync.dma_start(bias_o[:], b_o)
-        nc.sync.dma_start(pre_o[:, 0:HALF], xo[:, 0:HALF])
-
-        load_cw(sum(CW_LOADS[:3]), CW_LOADS[3])
-        load_cw(sum(CW_LOADS[:4]), CW_LOADS[4])
-        nc.sync.dma_start(pre_o[:, HALF:S], xo[:, HALF:S])
-
-        gate_f = held.tile([C, A], F32, name="gate_f")
-
-        def fw_on_vector(k):
-            fw = held.tile([C, PIECE], F32, name=f"fw{k}")
-            nc.vector.tensor_tensor(
-                fw[:].rearrange("c (t a) -> c t a", a=A),
-                child_w[:, k * PIECE : (k + 1) * PIECE].rearrange("c (t a) -> c t a", a=A),
-                gate_f[:].unsqueeze(1).to_broadcast([C, NODES, A]),
-                ALU.mult,
-            )
-            return fw
-
-        def fw_on_scalar(k):
-            slot_major = held.tile([C, A, NODES], F32, name=f"slot_major{k}")
-            by_slot = child_w[:, k * PIECE : (k + 1) * PIECE].rearrange("c (t a) -> c a t", a=A)
-            for a in range(A):
-                nc.scalar.activation(slot_major[:, a, :], by_slot[:, a, :], ACT.Copy, scale=gate_f[:, a : a + 1])
-            fw = held.tile([C, PIECE], F32, name=f"fw{k}")
-            nc.scalar.activation(
-                fw[:].rearrange("c (t a) -> c t a", a=A), slot_major[:].rearrange("c a t -> c t a"), ACT.Copy
-            )
-            return fw
+        nc.sync.dma_start(pre_o[:], xo)
 
         cell = held.tile([C, S], F32, name="cell")
         gate_i = held.tile([C, S], F32, name="gate_i")
@@ -108,59 +71,94 @@ def tile_batchedchildsumtreelstm_kernel(tc, xi, xo, xu, xf, b_i, b_o, b_u, b_f, 
             nc.scalar.activation(update[:, columns], pre_u[h][:], ACT.Tanh, bias=bias_u[:])
             nc.vector.tensor_tensor(cell[:, columns], gate_i[:, columns], update[:, columns], ALU.mult)
 
+        gate_f = held.tile([C, A], F32, name="gate_f")
         nc.scalar.activation(gate_f[:], pre_f[:], ACT.Sigmoid, bias=bias_f[:])
-        fws = {k: fw_on_scalar(k) for k in range(FW_AHEAD) if k % FW_VECTOR_EVERY != 0}
+
+        fw = held.tile([C, N], F32, name="fw")
+
+        def fw_on_vector(k):
+            entries = slice(k * PIECE, (k + 1) * PIECE)
+            nc.vector.tensor_tensor(
+                fw[:, entries].rearrange("c (t a) -> c t a", a=A),
+                child_w[:, entries].rearrange("c (t a) -> c t a", a=A),
+                gate_f[:].unsqueeze(1).to_broadcast([C, NODES, A]),
+                ALU.mult,
+            )
+
+        def fw_on_scalar(k):
+            entries = slice(k * PIECE, (k + 1) * PIECE)
+            slot_major = held.tile([C, A, NODES], F32, name=f"slot_major{k}")
+            by_slot = child_w[:, entries].rearrange("c (t a) -> c a t", a=A)
+            for a in range(A):
+                nc.scalar.activation(slot_major[:, a, :], by_slot[:, a, :], ACT.Copy, scale=gate_f[:, a : a + 1])
+            nc.scalar.activation(
+                fw[:, entries].rearrange("c (t a) -> c t a", a=A), slot_major[:].rearrange("c a t -> c t a"), ACT.Copy
+            )
+
+        product = held.tile([C, N], F32, name="product")
+
+        def look_up(k):
+            entries = slice(k * PIECE, (k + 1) * PIECE)
+            nc.vector.tensor_tensor(
+                product[:, entries],
+                cell[:].indirect(offsets[:, k * (PIECE // 16) : (k + 1) * (PIECE // 16)]),
+                fw[:, entries],
+                ALU.mult,
+            )
+
+        def sum_on_tensor(first_piece, pieces):
+            nodes = slice(first_piece * NODES, (first_piece + pieces) * NODES)
+            entries = slice(first_piece * PIECE, (first_piece + pieces) * PIECE)
+            state = sums.tile([C, pieces * NODES], F32, name=f"state{first_piece}")
+            nc.tensor.matmul(state[:], identity[:], cell[:, nodes], start=True, stop=False)
+            by_slot = product[:, entries].rearrange("c (t a) -> c a t", a=A)
+            for a in range(A):
+                nc.tensor.matmul(state[:], identity[:], by_slot[:, a, :], start=False, stop=(a == A - 1))
+            return state
+
+        def sum_on_vector(k):
+            nodes = slice(k * NODES, (k + 1) * NODES)
+            entries = slice(k * PIECE, (k + 1) * PIECE)
+            state = held.tile([C, NODES], F32, name=f"state{k}")
+            nc.vector.tensor_reduce(state[:], product[:, entries].rearrange("c (t a) -> c t a", a=A), AXIS.X, ALU.add)
+            nc.vector.tensor_tensor(state[:], state[:], cell[:, nodes], ALU.add)
+            return state
 
         gate_o = held.tile([C, S], F32, name="gate_o")
         hidden = held.tile([C, S], F32, name="hidden")
 
-        states = []
-        for k in range(PIECES - 1):
-            state = sums.tile([C, NODES], F32, name=f"state{k}")
-            nc.tensor.matmul(state[:], identity[:], cell[:, k * NODES : (k + 1) * NODES], start=True, stop=False)
-            states.append(state)
+        def squash(first_piece, state):
+            first = first_piece * NODES
+            if first % HALF == 0:
+                nc.scalar.activation(gate_o[:, first : first + HALF], pre_o[:, first : first + HALF], ACT.Sigmoid, bias=bias_o[:])
+            nc.scalar.activation(hidden[:, first : first + state.shape[1]], state[:], ACT.Tanh)
 
-        def sum_on_tensor(k, product):
-            by_slot = product[:].rearrange("c (t a) -> c a t", a=A)
-            for a in range(A):
-                nc.tensor.matmul(states[k][:], identity[:], by_slot[:, a, :], start=False, stop=(a == A - 1))
-            return states[k]
-
-        def sum_on_vector(k, product):
-            state = held.tile([C, NODES], F32, name=f"state{k}")
-            nc.vector.tensor_reduce(state[:], product[:].rearrange("c (t a) -> c t a", a=A), AXIS.X, ALU.add)
-            nc.vector.tensor_tensor(state[:], state[:], cell[:, k * NODES : (k + 1) * NODES], ALU.add)
-            return state
-
-        def squash(k):
-            nodes = slice(k * NODES, (k + 1) * NODES)
-            if (k * NODES) % HALF == 0:
-                half = slice(k * NODES, k * NODES + HALF)
-                nc.scalar.activation(gate_o[:, half], pre_o[:, half], ACT.Sigmoid, bias=bias_o[:])
-            nc.scalar.activation(hidden[:, nodes], summed[k][:], ACT.Tanh)
-
-        def finish(k):
-            nodes = slice(k * NODES, (k + 1) * NODES)
+        def finish(first_piece, state):
+            nodes = slice(first_piece * NODES, first_piece * NODES + state.shape[1])
             nc.vector.tensor_tensor(hidden[:, nodes], hidden[:, nodes], gate_o[:, nodes], ALU.mult)
             nc.sync.dma_start(out[:, nodes], hidden[:, nodes])
 
-        summed = []
-        for k in range(PIECES + LAG):
-            ahead = k + FW_AHEAD
-            if ahead < PIECES and ahead % FW_VECTOR_EVERY != 0:
-                fws[ahead] = fw_on_scalar(ahead)
-            if k < PIECES:
-                if k % FW_VECTOR_EVERY == 0:
-                    fws[k] = fw_on_vector(k)
-                product = held.tile([C, PIECE], F32, name=f"product{k}")
-                nc.vector.tensor_tensor(
-                    product[:],
-                    cell[:].indirect(offsets[:, k * (PIECE // 16) : (k + 1) * (PIECE // 16)]),
-                    fws[k][:],
-                    ALU.mult,
-                )
-                summed.append(sum_on_tensor(k, product) if k < PIECES - 1 else sum_on_vector(k, product))
-            if TANH_LAG <= k < PIECES + TANH_LAG:
-                squash(k - TANH_LAG)
-            if k >= LAG:
-                finish(k - LAG)
+        units = []
+        for k in range(EARLY):
+            fw_on_scalar(EARLY + k)
+            fw_on_vector(k)
+            look_up(k)
+            if k % 2 == 1:
+                units.append((k - 1, sum_on_tensor(k - 1, 2)))
+
+        squashed = 0
+        finished = 0
+        for k in range(EARLY, PIECES):
+            look_up(k)
+            units.append((k, sum_on_vector(k)))
+            squash(*units[squashed])
+            squashed += 1
+            if k > EARLY:
+                finish(*units[finished])
+                finished += 1
+        while finished < len(units):
+            if squashed < len(units):
+                squash(*units[squashed])
+                squashed += 1
+            finish(*units[finished])
+            finished += 1

@@ -17,7 +17,6 @@ NODES = PIECE // A
 EARLY = PIECES // 2
 CHUNK = 512
 CHUNKS = S // CHUNK
-HALF = S // 2
 
 
 def tile_batchedchildsumtreelstm_kernel(tc, xi, xo, xu, xf, b_i, b_o, b_u, b_f, cw, offs, out):
@@ -106,59 +105,64 @@ def tile_batchedchildsumtreelstm_kernel(tc, xi, xo, xu, xf, b_i, b_o, b_u, b_f, 
                 ALU.mult,
             )
 
-        def sum_on_tensor(first_piece, pieces):
-            nodes = slice(first_piece * NODES, (first_piece + pieces) * NODES)
-            entries = slice(first_piece * PIECE, (first_piece + pieces) * PIECE)
-            state = sums.tile([C, pieces * NODES], F32, name=f"state{first_piece}")
+        def open_sum_on_tensor(first_piece):
+            nodes = slice(first_piece * NODES, (first_piece + 2) * NODES)
+            state = sums.tile([C, 2 * NODES], F32, name=f"state{first_piece}")
             nc.tensor.matmul(state[:], identity[:], cell[:, nodes], start=True, stop=False)
+            return state
+
+        def sum_on_tensor(first_piece, state):
+            entries = slice(first_piece * PIECE, (first_piece + 2) * PIECE)
             by_slot = product[:, entries].rearrange("c (t a) -> c a t", a=A)
             for a in range(A):
                 nc.tensor.matmul(state[:], identity[:], by_slot[:, a, :], start=False, stop=(a == A - 1))
-            return state
 
-        def sum_on_vector(k):
-            nodes = slice(k * NODES, (k + 1) * NODES)
+        def add_products(k):
             entries = slice(k * PIECE, (k + 1) * PIECE)
             state = held.tile([C, NODES], F32, name=f"state{k}")
             nc.vector.tensor_reduce(state[:], product[:, entries].rearrange("c (t a) -> c t a", a=A), AXIS.X, ALU.add)
-            nc.vector.tensor_tensor(state[:], state[:], cell[:, nodes], ALU.add)
             return state
+
+        def add_cell(k, state):
+            nc.vector.tensor_tensor(state[:], state[:], cell[:, k * NODES : (k + 1) * NODES], ALU.add)
 
         gate_o = held.tile([C, S], F32, name="gate_o")
         hidden = held.tile([C, S], F32, name="hidden")
 
         def squash(first_piece, state):
-            first = first_piece * NODES
-            if first % HALF == 0:
-                nc.scalar.activation(gate_o[:, first : first + HALF], pre_o[:, first : first + HALF], ACT.Sigmoid, bias=bias_o[:])
-            nc.scalar.activation(hidden[:, first : first + state.shape[1]], state[:], ACT.Tanh)
+            nodes = slice(first_piece * NODES, first_piece * NODES + state.shape[1])
+            nc.scalar.activation(hidden[:, nodes], state[:], ACT.Tanh)
 
         def finish(first_piece, state):
             nodes = slice(first_piece * NODES, first_piece * NODES + state.shape[1])
             nc.vector.tensor_tensor(hidden[:, nodes], hidden[:, nodes], gate_o[:, nodes], ALU.mult)
             nc.sync.dma_start(out[:, nodes], hidden[:, nodes])
 
-        units = []
+
+        states = {first_piece: open_sum_on_tensor(first_piece) for first_piece in range(0, EARLY, 2)}
+        fw_on_vector(0)
         for k in range(EARLY):
             fw_on_scalar(EARLY + k)
-            fw_on_vector(k)
+            if k + 1 < EARLY:
+                fw_on_vector(k + 1)
             look_up(k)
             if k % 2 == 1:
-                units.append((k - 1, sum_on_tensor(k - 1, 2)))
+                sum_on_tensor(k - 1, states[k - 1])
 
-        squashed = 0
-        finished = 0
+        nc.scalar.activation(gate_o[:], pre_o[:], ACT.Sigmoid, bias=bias_o[:])
+        for first_piece in range(0, EARLY, 2):
+            squash(first_piece, states[first_piece])
+
+        for k in range(EARLY, PIECES + 2):
+            if k < PIECES:
+                look_up(k)
+            if EARLY <= k - 1 < PIECES:
+                states[k - 1] = add_products(k - 1)
+            if EARLY <= k - 2:
+                add_cell(k - 2, states[k - 2])
+                squash(k - 2, states[k - 2])
+            if k >= PIECES:
+                first_piece = 2 * (k - PIECES)
+                finish(first_piece, states[first_piece])
         for k in range(EARLY, PIECES):
-            look_up(k)
-            units.append((k, sum_on_vector(k)))
-            squash(*units[squashed])
-            squashed += 1
-            if k > EARLY:
-                finish(*units[finished])
-                finished += 1
-        while finished < len(units):
-            if squashed < len(units):
-                squash(*units[squashed])
-                squashed += 1
-            finish(*units[finished])
-            finished += 1
+            finish(k, states[k])

@@ -34,10 +34,8 @@ def tile_batchedchildsumtreelstm_kernel(tc, xi, xo, xu, xf, b_i, b_o, b_u, b_f, 
         pre_i = [held.tile([C, CHUNK], F32, name=f"pre_i{h}") for h in range(CHUNKS)]
         pre_u = [held.tile([C, CHUNK], F32, name=f"pre_u{h}") for h in range(CHUNKS)]
         nc.sync.dma_start(bias_i[:], b_i)
-        nc.sync.dma_start(pre_i[0][:], xi[:, 0:CHUNK])
         nc.sync.dma_start(bias_u[:], b_u)
-        nc.sync.dma_start(pre_u[0][:], xu[:, 0:CHUNK])
-        for h in range(1, CHUNKS):
+        for h in range(CHUNKS):
             columns = slice(h * CHUNK, (h + 1) * CHUNK)
             nc.sync.dma_start(pre_i[h][:], xi[:, columns])
             nc.sync.dma_start(pre_u[h][:], xu[:, columns])
@@ -49,9 +47,9 @@ def tile_batchedchildsumtreelstm_kernel(tc, xi, xo, xu, xf, b_i, b_o, b_u, b_f, 
 
         child_w = held.tile([C, N], F32, name="child_w")
         offsets = held.tile([C, N // 16], U16, name="offsets")
-        for k in range(EARLY):
-            for piece in (k, EARLY + k):
-                entries = slice(piece * PIECE, (piece + 1) * PIECE)
+        for k in range(0, EARLY, 2):
+            for first_piece in (k, EARLY + k):
+                entries = slice(first_piece * PIECE, (first_piece + 2) * PIECE)
                 nc.sync.dma_start(child_w[:, entries], cw[:, entries].rearrange("o n -> (o n)").partition_broadcast(C))
             if k == 0:
                 nc.sync.dma_start(offsets[:], offs)

@@ -15,6 +15,7 @@ PIECE = 512
 PIECES = N // PIECE
 NODES = PIECE // A
 EARLY = PIECES // 2
+FW_ON_VECTOR = 5
 CHUNK = 512
 CHUNKS = S // CHUNK
 
@@ -140,8 +141,9 @@ def tile_batchedchildsumtreelstm_kernel(tc, xi, xo, xu, xf, b_i, b_o, b_u, b_f, 
         states = {first_piece: open_sum_on_tensor(first_piece) for first_piece in range(0, EARLY, 2)}
         fw_on_vector(0)
         for k in range(EARLY):
-            fw_on_scalar(EARLY + k)
-            if k + 1 < EARLY:
+            if FW_ON_VECTOR + k < PIECES:
+                fw_on_scalar(FW_ON_VECTOR + k)
+            if k + 1 < FW_ON_VECTOR:
                 fw_on_vector(k + 1)
             look_up(k)
             if k % 2 == 1:

@@ -74,12 +74,12 @@ def tile_batchedchildsumtreelstm_kernel(tc, xi, xo, xu, xf, b_i, b_o, b_u, b_f, 
 
         fw = held.tile([C, N], F32, name="fw")
 
-        def fw_on_vector(k):
-            entries = slice(k * PIECE, (k + 1) * PIECE)
+        def fw_on_vector(first_piece, pieces):
+            entries = slice(first_piece * PIECE, (first_piece + pieces) * PIECE)
             nc.vector.tensor_tensor(
                 fw[:, entries].rearrange("c (t a) -> c t a", a=A),
                 child_w[:, entries].rearrange("c (t a) -> c t a", a=A),
-                gate_f[:].unsqueeze(1).to_broadcast([C, NODES, A]),
+                gate_f[:].unsqueeze(1).to_broadcast([C, pieces * NODES, A]),
                 ALU.mult,
             )
 
@@ -95,11 +95,11 @@ def tile_batchedchildsumtreelstm_kernel(tc, xi, xo, xu, xf, b_i, b_o, b_u, b_f, 
 
         product = held.tile([C, N], F32, name="product")
 
-        def look_up(k):
-            entries = slice(k * PIECE, (k + 1) * PIECE)
+        def look_up(first_piece, pieces):
+            entries = slice(first_piece * PIECE, (first_piece + pieces) * PIECE)
             nc.vector.tensor_tensor(
                 product[:, entries],
-                cell[:].indirect(offsets[:, k * (PIECE // 16) : (k + 1) * (PIECE // 16)]),
+                cell[:].indirect(offsets[:, first_piece * (PIECE // 16) : (first_piece + pieces) * (PIECE // 16)]),
                 fw[:, entries],
                 ALU.mult,
             )
@@ -139,15 +139,13 @@ def tile_batchedchildsumtreelstm_kernel(tc, xi, xo, xu, xf, b_i, b_o, b_u, b_f, 
 
 
         states = {first_piece: open_sum_on_tensor(first_piece) for first_piece in range(0, EARLY, 2)}
-        fw_on_vector(0)
-        for k in range(EARLY):
-            if FW_ON_VECTOR + k < PIECES:
-                fw_on_scalar(FW_ON_VECTOR + k)
-            if k + 1 < FW_ON_VECTOR:
-                fw_on_vector(k + 1)
-            look_up(k)
-            if k % 2 == 1:
-                sum_on_tensor(k - 1, states[k - 1])
+        fw_on_vector(0, 2)
+        for first_piece in range(0, EARLY, 2):
+            for k in range(FW_ON_VECTOR + first_piece, min(FW_ON_VECTOR + first_piece + 2, PIECES)):
+                fw_on_scalar(k)
+            fw_on_vector(first_piece + 2, min(2, FW_ON_VECTOR - first_piece - 2))
+            look_up(first_piece, 2)
+            sum_on_tensor(first_piece, states[first_piece])
 
         nc.scalar.activation(gate_o[:], pre_o[:], ACT.Sigmoid, bias=bias_o[:])
         for first_piece in range(0, EARLY, 2):
@@ -155,7 +153,7 @@ def tile_batchedchildsumtreelstm_kernel(tc, xi, xo, xu, xf, b_i, b_o, b_u, b_f, 
 
         for k in range(EARLY, PIECES + 2):
             if k < PIECES:
-                look_up(k)
+                look_up(k, 1)
             if EARLY <= k - 1 < PIECES:
                 states[k - 1] = add_products(k - 1)
             if EARLY <= k - 2:

@@ -49,11 +49,11 @@ def tile_batchedchildsumtreelstm_kernel(tc, xi, xo, xu, xf, b_i, b_o, b_u, b_f, 
         child_w = held.tile([C, N], F32, name="child_w")
         offsets = held.tile([C, N // 16], U16, name="offsets")
         for k in range(0, EARLY, 2):
+            if k == 0:
+                nc.sync.dma_start(offsets[:], offs)
             for first_piece in (k, EARLY + k):
                 entries = slice(first_piece * PIECE, (first_piece + 2) * PIECE)
                 nc.sync.dma_start(child_w[:, entries], cw[:, entries].rearrange("o n -> (o n)").partition_broadcast(C))
-            if k == 0:
-                nc.sync.dma_start(offsets[:], offs)
 
         bias_o = held.tile([C, 1], F32, name="bias_o")
         pre_o = held.tile([C, S], F32, name="pre_o")

@@ -34,12 +34,14 @@ def tile_batchedchildsumtreelstm_kernel(tc, xi, xo, xu, xf, b_i, b_o, b_u, b_f, 
         bias_u = held.tile([C, 1], F32, name="bias_u")
         pre_i = [held.tile([C, CHUNK], F32, name=f"pre_i{h}") for h in range(CHUNKS)]
         pre_u = [held.tile([C, CHUNK], F32, name=f"pre_u{h}") for h in range(CHUNKS)]
-        nc.sync.dma_start(bias_i[:], b_i)
-        nc.sync.dma_start(bias_u[:], b_u)
         for h in range(CHUNKS):
             columns = slice(h * CHUNK, (h + 1) * CHUNK)
             nc.sync.dma_start(pre_i[h][:], xi[:, columns])
+            if h == 0:
+                nc.sync.dma_start(bias_i[:], b_i)
             nc.sync.dma_start(pre_u[h][:], xu[:, columns])
+            if h == 0:
+                nc.sync.dma_start(bias_u[:], b_u)
 
         bias_f = held.tile([C, 1], F32, name="bias_f")
         pre_f = held.tile([C, A], F32, name="pre_f")

@@ -106,9 +106,9 @@ def tile_batchedchildsumtreelstm_kernel(tc, xi, xo, xu, xf, b_i, b_o, b_u, b_f, 
                 ALU.mult,
             )
 
-        def open_sum_on_tensor(first_piece):
-            nodes = slice(first_piece * NODES, (first_piece + 2) * NODES)
-            state = sums.tile([C, 2 * NODES], F32, name=f"state{first_piece}")
+        def open_sum_on_tensor(first_piece, pieces):
+            nodes = slice(first_piece * NODES, (first_piece + pieces) * NODES)
+            state = sums.tile([C, pieces * NODES], F32, name=f"state{first_piece}")
             nc.tensor.matmul(state[:], identity[:], cell[:, nodes], start=True, stop=False)
             return state
 
@@ -120,12 +120,15 @@ def tile_batchedchildsumtreelstm_kernel(tc, xi, xo, xu, xf, b_i, b_o, b_u, b_f, 
 
         def add_products(k):
             entries = slice(k * PIECE, (k + 1) * PIECE)
-            state = held.tile([C, NODES], F32, name=f"state{k}")
-            nc.vector.tensor_reduce(state[:], product[:, entries].rearrange("c (t a) -> c t a", a=A), AXIS.X, ALU.add)
-            return state
+            added = held.tile([C, NODES], F32, name=f"added{k}")
+            nc.vector.tensor_reduce(added[:], product[:, entries].rearrange("c (t a) -> c t a", a=A), AXIS.X, ALU.add)
+            return added
 
-        def add_cell(k, state):
-            nc.vector.tensor_tensor(state[:], state[:], cell[:, k * NODES : (k + 1) * NODES], ALU.add)
+        def close_sum_on_tensor(state, added):
+            nc.tensor.matmul(state[:], identity[:], added[:], start=False, stop=True)
+
+        def add_cell(k, added):
+            nc.vector.tensor_tensor(added[:], added[:], cell[:, k * NODES : (k + 1) * NODES], ALU.add)
 
         gate_o = held.tile([C, S], F32, name="gate_o")
         hidden = held.tile([C, S], F32, name="hidden")
@@ -140,7 +143,9 @@ def tile_batchedchildsumtreelstm_kernel(tc, xi, xo, xu, xf, b_i, b_o, b_u, b_f, 
             nc.sync.dma_start(out[:, nodes], hidden[:, nodes])
 
 
-        states = {first_piece: open_sum_on_tensor(first_piece) for first_piece in range(0, EARLY, 2)}
+        states = {first_piece: open_sum_on_tensor(first_piece, 2) for first_piece in range(0, EARLY, 2)}
+        for k in range(EARLY, PIECES - 1):
+            states[k] = open_sum_on_tensor(k, 1)
         fw_on_vector(0, 2)
         for first_piece in range(0, EARLY, 2):
             for k in range(FW_ON_VECTOR + first_piece, min(FW_ON_VECTOR + first_piece + 2, PIECES)):
@@ -153,16 +158,16 @@ def tile_batchedchildsumtreelstm_kernel(tc, xi, xo, xu, xf, b_i, b_o, b_u, b_f, 
         for first_piece in range(0, EARLY, 2):
             squash(first_piece, states[first_piece])
 
-        for k in range(EARLY, PIECES + 2):
-            if k < PIECES:
-                look_up(k, 1)
-            if EARLY <= k - 1 < PIECES:
-                states[k - 1] = add_products(k - 1)
-            if EARLY <= k - 2:
-                add_cell(k - 2, states[k - 2])
-                squash(k - 2, states[k - 2])
-            if k >= PIECES:
-                first_piece = 2 * (k - PIECES)
-                finish(first_piece, states[first_piece])
+        for k in range(EARLY, PIECES):
+            look_up(k, 1)
+            if k > EARLY:
+                close_sum_on_tensor(states[k - 1], add_products(k - 1))
+                squash(k - 1, states[k - 1])
+        last = PIECES - 1
+        states[last] = add_products(last)
+        finish(0, states[0])
+        add_cell(last, states[last])
+        squash(last, states[last])
+        finish(2, states[2])
         for k in range(EARLY, PIECES):
             finish(k, states[k])

import concourse.mybir as mybir
from concourse.masks import make_identity

F32 = mybir.dt.float32
U16 = mybir.dt.uint16
ACT = mybir.ActivationFunctionType
ALU = mybir.AluOpType
AXIS = mybir.AxisListType

C = 128
S = 1024
A = 4
N = S * A
PIECE = 512
PIECES = N // PIECE
NODES = PIECE // A
EARLY = PIECES // 2
FW_ON_VECTOR = 5
CHUNK = 512
CHUNKS = S // CHUNK


def tile_batchedchildsumtreelstm_kernel(tc, xi, xo, xu, xf, b_i, b_o, b_u, b_f, cw, offs, out):
    nc = tc.nc
    with tc.tile_pool(name="held", bufs=1) as held, tc.psum_pool(name="sums", bufs=1) as sums:
        warm = held.tile([C, 1], F32, name="warm")
        nc.vector.memset(warm[:], 0.0)
        nc.scalar.activation(warm[:], warm[:], ACT.Sigmoid)

        identity = held.tile([C, C], F32, name="identity")
        make_identity(nc, identity[:])

        bias_i = held.tile([C, 1], F32, name="bias_i")
        bias_u = held.tile([C, 1], F32, name="bias_u")
        pre_i = [held.tile([C, CHUNK], F32, name=f"pre_i{h}") for h in range(CHUNKS)]
        pre_u = [held.tile([C, CHUNK], F32, name=f"pre_u{h}") for h in range(CHUNKS)]
        for h in range(CHUNKS):
            columns = slice(h * CHUNK, (h + 1) * CHUNK)
            nc.sync.dma_start(pre_i[h][:], xi[:, columns])
            if h == 0:
                nc.sync.dma_start(bias_i[:], b_i)
            nc.sync.dma_start(pre_u[h][:], xu[:, columns])
            if h == 0:
                nc.sync.dma_start(bias_u[:], b_u)

        bias_f = held.tile([C, 1], F32, name="bias_f")
        pre_f = held.tile([C, A], F32, name="pre_f")
        nc.sync.dma_start(bias_f[:], b_f)
        nc.sync.dma_start(pre_f[:], xf)

        child_w = held.tile([C, N], F32, name="child_w")
        offsets = held.tile([C, N // 16], U16, name="offsets")
        for k in range(0, EARLY, 2):
            if k == 0:
                nc.sync.dma_start(offsets[:], offs)
            for first_piece in (k, EARLY + k):
                entries = slice(first_piece * PIECE, (first_piece + 2) * PIECE)
                nc.sync.dma_start(child_w[:, entries], cw[:, entries].rearrange("o n -> (o n)").partition_broadcast(C))

        bias_o = held.tile([C, 1], F32, name="bias_o")
        pre_o = held.tile([C, S], F32, name="pre_o")
        nc.sync.dma_start(bias_o[:], b_o)
        nc.sync.dma_start(pre_o[:], xo)

        cell = held.tile([C, S], F32, name="cell")
        gate_i = held.tile([C, S], F32, name="gate_i")
        update = held.tile([C, S], F32, name="update")
        for h in range(CHUNKS):
            columns = slice(h * CHUNK, (h + 1) * CHUNK)
            nc.scalar.activation(gate_i[:, columns], pre_i[h][:], ACT.Sigmoid, bias=bias_i[:])
            nc.scalar.activation(update[:, columns], pre_u[h][:], ACT.Tanh, bias=bias_u[:])
            nc.vector.tensor_tensor(cell[:, columns], gate_i[:, columns], update[:, columns], ALU.mult)

        gate_f = held.tile([C, A], F32, name="gate_f")
        nc.scalar.activation(gate_f[:], pre_f[:], ACT.Sigmoid, bias=bias_f[:])

        fw = held.tile([C, N], F32, name="fw")

        def fw_on_vector(first_piece, pieces):
            entries = slice(first_piece * PIECE, (first_piece + pieces) * PIECE)
            nc.vector.tensor_tensor(
                fw[:, entries].rearrange("c (t a) -> c t a", a=A),
                child_w[:, entries].rearrange("c (t a) -> c t a", a=A),
                gate_f[:].unsqueeze(1).to_broadcast([C, pieces * NODES, A]),
                ALU.mult,
            )

        def fw_on_scalar(k):
            entries = slice(k * PIECE, (k + 1) * PIECE)
            slot_major = held.tile([C, A, NODES], F32, name=f"slot_major{k}")
            by_slot = child_w[:, entries].rearrange("c (t a) -> c a t", a=A)
            for a in range(A):
                nc.scalar.activation(slot_major[:, a, :], by_slot[:, a, :], ACT.Copy, scale=gate_f[:, a : a + 1])
            nc.scalar.activation(
                fw[:, entries].rearrange("c (t a) -> c t a", a=A), slot_major[:].rearrange("c a t -> c t a"), ACT.Copy
            )

        product = held.tile([C, N], F32, name="product")

        def look_up(first_piece, pieces):
            entries = slice(first_piece * PIECE, (first_piece + pieces) * PIECE)
            nc.vector.tensor_tensor(
                product[:, entries],
                cell[:].indirect(offsets[:, first_piece * (PIECE // 16) : (first_piece + pieces) * (PIECE // 16)]),
                fw[:, entries],
                ALU.mult,
            )

        def open_sum_on_tensor(first_piece, pieces):
            nodes = slice(first_piece * NODES, (first_piece + pieces) * NODES)
            state = sums.tile([C, pieces * NODES], F32, name=f"state{first_piece}")
            nc.tensor.matmul(state[:], identity[:], cell[:, nodes], start=True, stop=False)
            return state

        def sum_on_tensor(first_piece, state):
            entries = slice(first_piece * PIECE, (first_piece + 2) * PIECE)
            by_slot = product[:, entries].rearrange("c (t a) -> c a t", a=A)
            for a in range(A):
                nc.tensor.matmul(state[:], identity[:], by_slot[:, a, :], start=False, stop=(a == A - 1))

        def add_products(k):
            entries = slice(k * PIECE, (k + 1) * PIECE)
            added = held.tile([C, NODES], F32, name=f"added{k}")
            nc.vector.tensor_reduce(added[:], product[:, entries].rearrange("c (t a) -> c t a", a=A), AXIS.X, ALU.add)
            return added

        def close_sum_on_tensor(state, added):
            nc.tensor.matmul(state[:], identity[:], added[:], start=False, stop=True)

        def add_cell(k, added):
            nc.vector.tensor_tensor(added[:], added[:], cell[:, k * NODES : (k + 1) * NODES], ALU.add)

        gate_o = held.tile([C, S], F32, name="gate_o")
        hidden = held.tile([C, S], F32, name="hidden")

        def squash(first_piece, state):
            nodes = slice(first_piece * NODES, first_piece * NODES + state.shape[1])
            nc.scalar.activation(hidden[:, nodes], state[:], ACT.Tanh)

        def finish(first_piece, state):
            nodes = slice(first_piece * NODES, first_piece * NODES + state.shape[1])
            nc.vector.tensor_tensor(hidden[:, nodes], hidden[:, nodes], gate_o[:, nodes], ALU.mult)
            nc.sync.dma_start(out[:, nodes], hidden[:, nodes])


        states = {first_piece: open_sum_on_tensor(first_piece, 2) for first_piece in range(0, EARLY, 2)}
        for k in range(EARLY, PIECES - 1):
            states[k] = open_sum_on_tensor(k, 1)
        fw_on_vector(0, 2)
        for first_piece in range(0, EARLY, 2):
            for k in range(FW_ON_VECTOR + first_piece, min(FW_ON_VECTOR + first_piece + 2, PIECES)):
                fw_on_scalar(k)
            fw_on_vector(first_piece + 2, min(2, FW_ON_VECTOR - first_piece - 2))
            look_up(first_piece, 2)
            sum_on_tensor(first_piece, states[first_piece])

        nc.scalar.activation(gate_o[:], pre_o[:], ACT.Sigmoid, bias=bias_o[:])
        for first_piece in range(0, EARLY, 2):
            squash(first_piece, states[first_piece])

        for k in range(EARLY, PIECES):
            look_up(k, 1)
            if k > EARLY:
                close_sum_on_tensor(states[k - 1], add_products(k - 1))
                squash(k - 1, states[k - 1])
        last = PIECES - 1
        states[last] = add_products(last)
        finish(0, states[0])
        add_cell(last, states[last])
        squash(last, states[last])
        finish(2, states[2])
        for k in range(EARLY, PIECES):
            finish(k, states[k])
